import numpy as np
import ml_dtypes

BF16 = ml_dtypes.bfloat16


def bf(x):
    return np.asarray(x, np.float32).astype(BF16)


def f32(x):
    return np.asarray(x, np.float32)


def f64(x):
    return np.asarray(x).astype(np.float64)


def striped(idx):
    return np.tile(idx.reshape(-1, 16).T, (8, 1))


C, S, N = 512, 2048, 2048


def setup_inputs():
    return {"x": f32(np.random.standard_normal((C, S))), "scale_a": f32(np.random.standard_normal((1, S))), "scale_b": f32(np.random.standard_normal((1, N))), "offs": striped(np.random.permutation(S)[:N])}


def reference(x, scale_a, scale_b, offs):
    idx = offs[:16].T.reshape(-1)
    y = f64(x) * f64(scale_a)
    return y[:, idx] * f64(scale_b)

@@ -1,0 +1,37 @@
+import concourse.mybir as mybir
+
+P = 128
+TOKENS = 512
+FEATURES = 2048
+BLOCKS = TOKENS // P
+
+F32 = mybir.dt.float32
+U16 = mybir.dt.uint16
+MULT = mybir.AluOpType.mult
+
+
+def tile_monarchlinearlayer_kernel(tc, x, scale_a, scale_b, offs, out):
+    nc = tc.nc
+    with (
+        tc.tile_pool(name="held", bufs=1) as held,
+        tc.tile_pool(name="blocks", bufs=BLOCKS) as blocks,
+    ):
+        offsets = held.tile([P, FEATURES // 16], U16, name="offsets")
+        nc.sync.dma_start(offsets[:], offs)
+
+        factor_a = held.tile([P, FEATURES], F32, name="factor_a")
+        nc.scalar.dma_start(factor_a[:], scale_a.squeeze(0).partition_broadcast(P))
+        factor_b = held.tile([P, FEATURES], F32, name="factor_b")
+        nc.scalar.dma_start(factor_b[:], scale_b.squeeze(0).partition_broadcast(P))
+
+        for b in range(BLOCKS):
+            rows = slice(b * P, (b + 1) * P)
+            x_block = blocks.tile([P, FEATURES], F32, name="x_block")
+            nc.sync.dma_start(x_block[:], x[rows, :])
+
+            y_block = blocks.tile([P, FEATURES], F32, name="y_block")
+            nc.vector.tensor_tensor(y_block[:], x_block[:], factor_a[:], MULT)
+
+            out_block = blocks.tile([P, FEATURES], F32, name="out_block")
+            nc.vector.tensor_tensor(out_block[:], y_block[:].indirect(offsets[:]), factor_b[:], MULT)
+            nc.scalar.dma_start(out[rows, :], out_block[:])

@@ -30,7 +30,8 @@ def tile_monarchlinearlayer_kernel(tc, x, scale_a, scale_b, offs, out):
             nc.sync.dma_start(x_block[:], x[rows, :])
 
             y_block = blocks.tile([P, FEATURES], F32, name="y_block")
-            nc.vector.tensor_tensor(y_block[:], x_block[:], factor_a[:], MULT)
+            first_stage_engine = nc.vector if b == 0 else nc.gpsimd
+            first_stage_engine.tensor_tensor(y_block[:], x_block[:], factor_a[:], MULT)
 
             out_block = blocks.tile([P, FEATURES], F32, name="out_block")
             nc.vector.tensor_tensor(out_block[:], y_block[:].indirect(offsets[:]), factor_b[:], MULT)

@@ -4,6 +4,8 @@ P = 128
 TOKENS = 512
 FEATURES = 2048
 BLOCKS = TOKENS // P
+CHUNK = 512
+CHUNKS = FEATURES // CHUNK
 
 F32 = mybir.dt.float32
 U16 = mybir.dt.uint16
@@ -12,27 +14,39 @@ MULT = mybir.AluOpType.mult
 
 def tile_monarchlinearlayer_kernel(tc, x, scale_a, scale_b, offs, out):
     nc = tc.nc
-    with (
-        tc.tile_pool(name="held", bufs=1) as held,
-        tc.tile_pool(name="blocks", bufs=BLOCKS) as blocks,
-    ):
-        offsets = held.tile([P, FEATURES // 16], U16, name="offsets")
-        nc.sync.dma_start(offsets[:], offs)
+    row_a = scale_a.squeeze(0)
+    row_b = scale_b.squeeze(0)
 
+    with tc.tile_pool(name="held", bufs=1) as held:
+        offsets = held.tile([P, FEATURES // 16], U16, name="offsets")
         factor_a = held.tile([P, FEATURES], F32, name="factor_a")
-        nc.scalar.dma_start(factor_a[:], scale_a.squeeze(0).partition_broadcast(P))
         factor_b = held.tile([P, FEATURES], F32, name="factor_b")
-        nc.scalar.dma_start(factor_b[:], scale_b.squeeze(0).partition_broadcast(P))
+        x_blocks = [held.tile([P, FEATURES], F32, name=f"x_block{b}") for b in range(BLOCKS)]
+        y_blocks = [held.tile([P, FEATURES], F32, name=f"y_block{b}") for b in range(BLOCKS)]
+        out_blocks = [held.tile([P, FEATURES], F32, name=f"out_block{b}") for b in range(BLOCKS)]
+
+        for c in range(CHUNKS):
+            cols = slice(c * CHUNK, (c + 1) * CHUNK)
+            nc.sync.dma_start(x_blocks[0][:, cols], x[0:P, cols])
+            nc.sync.dma_start(factor_a[:, cols], row_a[cols].partition_broadcast(P))
+        nc.sync.dma_start(offsets[:], offs)
+        nc.sync.dma_start(factor_b[:, 0:CHUNK], row_b[0:CHUNK].partition_broadcast(P))
+        nc.sync.dma_start(factor_b[:, CHUNK:FEATURES], row_b[CHUNK:FEATURES].partition_broadcast(P))
+        for b in range(1, BLOCKS):
+            nc.sync.dma_start(x_blocks[b][:], x[b * P : (b + 1) * P, :])
 
         for b in range(BLOCKS):
-            rows = slice(b * P, (b + 1) * P)
-            x_block = blocks.tile([P, FEATURES], F32, name="x_block")
-            nc.sync.dma_start(x_block[:], x[rows, :])
+            width = CHUNK if b == 0 else FEATURES
+            for start in range(0, FEATURES, width):
+                cols = slice(start, start + width)
+                nc.vector.tensor_tensor(y_blocks[b][:, cols], x_blocks[b][:, cols], factor_a[:, cols], MULT)
 
-            y_block = blocks.tile([P, FEATURES], F32, name="y_block")
-            first_stage_engine = nc.vector if b == 0 else nc.gpsimd
-            first_stage_engine.tensor_tensor(y_block[:], x_block[:], factor_a[:], MULT)
-
-            out_block = blocks.tile([P, FEATURES], F32, name="out_block")
-            nc.vector.tensor_tensor(out_block[:], y_block[:].indirect(offsets[:]), factor_b[:], MULT)
-            nc.scalar.dma_start(out[rows, :], out_block[:])
+            cuts = [0, CHUNK, FEATURES] if b == 0 else [0, FEATURES]
+            for start, end in zip(cuts[:-1], cuts[1:]):
+                nc.vector.tensor_tensor(
+                    out_blocks[b][:, start:end],
+                    y_blocks[b][:].indirect(offsets[:, start // 16 : end // 16]),
+                    factor_b[:, start:end],
+                    MULT,
+                )
+            nc.scalar.dma_start(out[b * P : (b + 1) * P, :], out_blocks[b][:])

@@ -4,8 +4,7 @@ P = 128
 TOKENS = 512
 FEATURES = 2048
 BLOCKS = TOKENS // P
-CHUNK = 512
-CHUNKS = FEATURES // CHUNK
+LAST_PIECE = 512
 
 F32 = mybir.dt.float32
 U16 = mybir.dt.uint16
@@ -14,39 +13,33 @@ MULT = mybir.AluOpType.mult
 
 def tile_monarchlinearlayer_kernel(tc, x, scale_a, scale_b, offs, out):
     nc = tc.nc
-    row_a = scale_a.squeeze(0)
-    row_b = scale_b.squeeze(0)
-
-    with tc.tile_pool(name="held", bufs=1) as held:
+    with (
+        tc.tile_pool(name="held", bufs=1) as held,
+        tc.tile_pool(name="blocks", bufs=BLOCKS) as blocks,
+    ):
         offsets = held.tile([P, FEATURES // 16], U16, name="offsets")
-        factor_a = held.tile([P, FEATURES], F32, name="factor_a")
-        factor_b = held.tile([P, FEATURES], F32, name="factor_b")
-        x_blocks = [held.tile([P, FEATURES], F32, name=f"x_block{b}") for b in range(BLOCKS)]
-        y_blocks = [held.tile([P, FEATURES], F32, name=f"y_block{b}") for b in range(BLOCKS)]
-        out_blocks = [held.tile([P, FEATURES], F32, name=f"out_block{b}") for b in range(BLOCKS)]
-
-        for c in range(CHUNKS):
-            cols = slice(c * CHUNK, (c + 1) * CHUNK)
-            nc.sync.dma_start(x_blocks[0][:, cols], x[0:P, cols])
-            nc.sync.dma_start(factor_a[:, cols], row_a[cols].partition_broadcast(P))
         nc.sync.dma_start(offsets[:], offs)
-        nc.sync.dma_start(factor_b[:, 0:CHUNK], row_b[0:CHUNK].partition_broadcast(P))
-        nc.sync.dma_start(factor_b[:, CHUNK:FEATURES], row_b[CHUNK:FEATURES].partition_broadcast(P))
-        for b in range(1, BLOCKS):
-            nc.sync.dma_start(x_blocks[b][:], x[b * P : (b + 1) * P, :])
+
+        factor_a = held.tile([P, FEATURES], F32, name="factor_a")
+        nc.scalar.dma_start(factor_a[:], scale_a.squeeze(0).partition_broadcast(P))
+        factor_b = held.tile([P, FEATURES], F32, name="factor_b")
+        nc.scalar.dma_start(factor_b[:], scale_b.squeeze(0).partition_broadcast(P))
 
         for b in range(BLOCKS):
-            width = CHUNK if b == 0 else FEATURES
-            for start in range(0, FEATURES, width):
-                cols = slice(start, start + width)
-                nc.vector.tensor_tensor(y_blocks[b][:, cols], x_blocks[b][:, cols], factor_a[:, cols], MULT)
+            rows = slice(b * P, (b + 1) * P)
+            x_block = blocks.tile([P, FEATURES], F32, name="x_block")
+            nc.sync.dma_start(x_block[:], x[rows, :])
 
-            cuts = [0, CHUNK, FEATURES] if b == 0 else [0, FEATURES]
+            y_block = blocks.tile([P, FEATURES], F32, name="y_block")
+            nc.vector.tensor_tensor(y_block[:], x_block[:], factor_a[:], MULT)
+
+            out_block = blocks.tile([P, FEATURES], F32, name="out_block")
+            cuts = [0, FEATURES - LAST_PIECE, FEATURES] if b == BLOCKS - 1 else [0, FEATURES]
             for start, end in zip(cuts[:-1], cuts[1:]):
                 nc.vector.tensor_tensor(
-                    out_blocks[b][:, start:end],
-                    y_blocks[b][:].indirect(offsets[:, start // 16 : end // 16]),
+                    out_block[:, start:end],
+                    y_block[:].indirect(offsets[:, start // 16 : end // 16]),
                     factor_b[:, start:end],
                     MULT,
                 )
-            nc.scalar.dma_start(out[b * P : (b + 1) * P, :], out_blocks[b][:])
+                nc.scalar.dma_start(out[rows, start:end], out_block[:, start:end])

@@ -18,20 +18,22 @@ def tile_monarchlinearlayer_kernel(tc, x, scale_a, scale_b, offs, out):
         tc.tile_pool(name="blocks", bufs=BLOCKS) as blocks,
     ):
         offsets = held.tile([P, FEATURES // 16], U16, name="offsets")
-        nc.sync.dma_start(offsets[:], offs)
-
         factor_a = held.tile([P, FEATURES], F32, name="factor_a")
-        nc.scalar.dma_start(factor_a[:], scale_a.squeeze(0).partition_broadcast(P))
         factor_b = held.tile([P, FEATURES], F32, name="factor_b")
-        nc.scalar.dma_start(factor_b[:], scale_b.squeeze(0).partition_broadcast(P))
+        x_blocks = [blocks.tile([P, FEATURES], F32, name="x_block") for b in range(BLOCKS)]
+
+        nc.scalar.dma_start(factor_a[:], scale_a.squeeze(0).partition_broadcast(P))
+        nc.sync.dma_start(x_blocks[0][:], x[0:P, :])
+        nc.sync.dma_start(offsets[:], offs)
+        nc.sync.dma_start(factor_b[:], scale_b.squeeze(0).partition_broadcast(P))
+        for b in range(1, BLOCKS):
+            nc.sync.dma_start(x_blocks[b][:], x[b * P : (b + 1) * P, :])
 
         for b in range(BLOCKS):
             rows = slice(b * P, (b + 1) * P)
-            x_block = blocks.tile([P, FEATURES], F32, name="x_block")
-            nc.sync.dma_start(x_block[:], x[rows, :])
 
             y_block = blocks.tile([P, FEATURES], F32, name="y_block")
-            nc.vector.tensor_tensor(y_block[:], x_block[:], factor_a[:], MULT)
+            nc.vector.tensor_tensor(y_block[:], x_blocks[b][:], factor_a[:], MULT)
 
             out_block = blocks.tile([P, FEATURES], F32, name="out_block")
             cuts = [0, FEATURES - LAST_PIECE, FEATURES] if b == BLOCKS - 1 else [0, FEATURES]

@@ -5,6 +5,7 @@ TOKENS = 512
 FEATURES = 2048
 BLOCKS = TOKENS // P
 LAST_PIECE = 512
+HALF = FEATURES // 2
 
 F32 = mybir.dt.float32
 U16 = mybir.dt.uint16
@@ -13,6 +14,8 @@ MULT = mybir.AluOpType.mult
 
 def tile_monarchlinearlayer_kernel(tc, x, scale_a, scale_b, offs, out):
     nc = tc.nc
+    row_a = scale_a.squeeze(0)
+    row_b = scale_b.squeeze(0)
     with (
         tc.tile_pool(name="held", bufs=1) as held,
         tc.tile_pool(name="blocks", bufs=BLOCKS) as blocks,
@@ -22,12 +25,17 @@ def tile_monarchlinearlayer_kernel(tc, x, scale_a, scale_b, offs, out):
         factor_b = held.tile([P, FEATURES], F32, name="factor_b")
         x_blocks = [blocks.tile([P, FEATURES], F32, name="x_block") for b in range(BLOCKS)]
 
-        nc.scalar.dma_start(factor_a[:], scale_a.squeeze(0).partition_broadcast(P))
-        nc.sync.dma_start(x_blocks[0][:], x[0:P, :])
+        halves = [(nc.sync, slice(0, HALF)), (nc.scalar, slice(HALF, FEATURES))]
+        for queue, cols in halves:
+            queue.dma_start(factor_a[:, cols], row_a[cols].partition_broadcast(P))
+        for queue, cols in halves:
+            queue.dma_start(x_blocks[0][:, cols], x[0:P, cols])
         nc.sync.dma_start(offsets[:], offs)
-        nc.sync.dma_start(factor_b[:], scale_b.squeeze(0).partition_broadcast(P))
+        for queue, cols in halves:
+            queue.dma_start(factor_b[:, cols], row_b[cols].partition_broadcast(P))
         for b in range(1, BLOCKS):
-            nc.sync.dma_start(x_blocks[b][:], x[b * P : (b + 1) * P, :])
+            for queue, cols in halves:
+                queue.dma_start(x_blocks[b][:, cols], x[b * P : (b + 1) * P, cols])
 
         for b in range(BLOCKS):
             rows = slice(b * P, (b + 1) * P)

@@ -1,47 +1,70 @@
 import concourse.mybir as mybir
+from concourse.masks import make_identity
 
 P = 128
 TOKENS = 512
 FEATURES = 2048
 BLOCKS = TOKENS // P
 LAST_PIECE = 512
-HALF = FEATURES // 2
+BANK = 512
+SQUARES = BANK // P
 
 F32 = mybir.dt.float32
 U16 = mybir.dt.uint16
 MULT = mybir.AluOpType.mult
+COPY = mybir.ActivationFunctionType.Copy
 
 
 def tile_monarchlinearlayer_kernel(tc, x, scale_a, scale_b, offs, out):
     nc = tc.nc
-    row_a = scale_a.squeeze(0)
-    row_b = scale_b.squeeze(0)
     with (
         tc.tile_pool(name="held", bufs=1) as held,
         tc.tile_pool(name="blocks", bufs=BLOCKS) as blocks,
+        tc.tile_pool(name="work", bufs=2) as work,
+        tc.psum_pool(name="psum", bufs=2) as psum,
     ):
         offsets = held.tile([P, FEATURES // 16], U16, name="offsets")
         factor_a = held.tile([P, FEATURES], F32, name="factor_a")
         factor_b = held.tile([P, FEATURES], F32, name="factor_b")
         x_blocks = [blocks.tile([P, FEATURES], F32, name="x_block") for b in range(BLOCKS)]
 
-        halves = [(nc.sync, slice(0, HALF)), (nc.scalar, slice(HALF, FEATURES))]
-        for queue, cols in halves:
-            queue.dma_start(factor_a[:, cols], row_a[cols].partition_broadcast(P))
-        for queue, cols in halves:
-            queue.dma_start(x_blocks[0][:, cols], x[0:P, cols])
+        nc.scalar.dma_start(factor_a[:], scale_a.squeeze(0).partition_broadcast(P))
+        nc.sync.dma_start(x_blocks[0][:], x[0:P, :])
         nc.sync.dma_start(offsets[:], offs)
-        for queue, cols in halves:
-            queue.dma_start(factor_b[:, cols], row_b[cols].partition_broadcast(P))
+        nc.sync.dma_start(factor_b[:], scale_b.squeeze(0).partition_broadcast(P))
         for b in range(1, BLOCKS):
-            for queue, cols in halves:
-                queue.dma_start(x_blocks[b][:, cols], x[b * P : (b + 1) * P, cols])
+            nc.sync.dma_start(x_blocks[b][:], x[b * P : (b + 1) * P, :])
+
+        identity = held.tile([P, P], F32, name="identity")
+        make_identity(nc, identity[:])
+        a_rows = held.tile([P, P], F32, name="a_rows")
+        nc.gpsimd.memset(a_rows[:], 0.0)
+        nc.scalar.dma_start(a_rows[0 : FEATURES // P, :], scale_a.squeeze(0).rearrange("(j p) -> j p", p=P))
+        a_flipped = psum.tile([P, P], F32, name="a_flipped")
+        nc.tensor.transpose(a_flipped[:], a_rows[:], identity[:])
+        a_columns = held.tile([P, P], F32, name="a_columns")
+        nc.scalar.activation(a_columns[:], a_flipped[:], COPY)
 
         for b in range(BLOCKS):
             rows = slice(b * P, (b + 1) * P)
-
             y_block = blocks.tile([P, FEATURES], F32, name="y_block")
-            nc.vector.tensor_tensor(y_block[:], x_blocks[b][:], factor_a[:], MULT)
+
+            on_vector = FEATURES // 4 if b >= 2 else FEATURES
+            nc.vector.tensor_tensor(
+                y_block[:, 0:on_vector], x_blocks[b][:, 0:on_vector], factor_a[:, 0:on_vector], MULT
+            )
+            for start in range(on_vector, FEATURES, BANK):
+                squares = [(k, slice(k * P, (k + 1) * P), start // P + k) for k in range(SQUARES)]
+                flipped = psum.tile([P, BANK], F32, name="flipped")
+                for k, part, j in squares:
+                    nc.tensor.transpose(flipped[:, part], x_blocks[b][:, j * P : (j + 1) * P], identity[:])
+                scaled = work.tile([P, BANK], F32, name="scaled")
+                for k, part, j in squares:
+                    nc.scalar.activation(scaled[:, part], flipped[:, part], COPY, scale=a_columns[:, j : j + 1])
+                back = psum.tile([P, BANK], F32, name="back")
+                for k, part, j in squares:
+                    nc.tensor.transpose(back[:, part], scaled[:, part], identity[:])
+                nc.scalar.activation(y_block[:, start : start + BANK], back[:], COPY)
 
             out_block = blocks.tile([P, FEATURES], F32, name="out_block")
             cuts = [0, FEATURES - LAST_PIECE, FEATURES] if b == BLOCKS - 1 else [0, FEATURES]
@@ -52,4 +75,4 @@ def tile_monarchlinearlayer_kernel(tc, x, scale_a, scale_b, offs, out):
                     factor_b[:, start:end],
                     MULT,
                 )
-                nc.scalar.dma_start(out[rows, start:end], out_block[:, start:end])
+                nc.sync.dma_start(out[rows, start:end], out_block[:, start:end])

@@ -49,10 +49,11 @@ def tile_monarchlinearlayer_kernel(tc, x, scale_a, scale_b, offs, out):
             rows = slice(b * P, (b + 1) * P)
             y_block = blocks.tile([P, FEATURES], F32, name="y_block")
 
-            on_vector = FEATURES // 4 if b >= 2 else FEATURES
-            nc.vector.tensor_tensor(
-                y_block[:, 0:on_vector], x_blocks[b][:, 0:on_vector], factor_a[:, 0:on_vector], MULT
-            )
+            on_vector = 0 if b >= 2 else FEATURES
+            if on_vector > 0:
+                nc.vector.tensor_tensor(
+                    y_block[:, 0:on_vector], x_blocks[b][:, 0:on_vector], factor_a[:, 0:on_vector], MULT
+                )
             for start in range(on_vector, FEATURES, BANK):
                 squares = [(k, slice(k * P, (k + 1) * P), start // P + k) for k in range(SQUARES)]
                 flipped = psum.tile([P, BANK], F32, name="flipped")

@@ -7,7 +7,11 @@ FEATURES = 2048
 BLOCKS = TOKENS // P
 LAST_PIECE = 512
 BANK = 512
+BANKS = 8
+CHUNKS = FEATURES // BANK
 SQUARES = BANK // P
+GROUPS = FEATURES // P
+LAG = 2
 
 F32 = mybir.dt.float32
 U16 = mybir.dt.uint16
@@ -20,52 +24,77 @@ def tile_monarchlinearlayer_kernel(tc, x, scale_a, scale_b, offs, out):
     with (
         tc.tile_pool(name="held", bufs=1) as held,
         tc.tile_pool(name="blocks", bufs=BLOCKS) as blocks,
-        tc.tile_pool(name="work", bufs=2) as work,
-        tc.psum_pool(name="psum", bufs=2) as psum,
+        tc.tile_pool(name="work", bufs=LAG + 1) as work,
+        tc.psum_pool(name="psum", bufs=BANKS) as psum,
     ):
         offsets = held.tile([P, FEATURES // 16], U16, name="offsets")
-        factor_a = held.tile([P, FEATURES], F32, name="factor_a")
-        factor_b = held.tile([P, FEATURES], F32, name="factor_b")
         x_blocks = [blocks.tile([P, FEATURES], F32, name="x_block") for b in range(BLOCKS)]
 
+        factor_rows = held.tile([P, P], F32, name="factor_rows")
+        nc.vector.memset(factor_rows[2 * GROUPS : 4 * GROUPS, :], 0.0)
+        nc.vector.memset(factor_rows[4 * GROUPS : P, :], 0.0)
+        nc.sync.dma_start(factor_rows[0:GROUPS, :], scale_a.squeeze(0).rearrange("(j p) -> j p", p=P))
+        nc.scalar.dma_start(factor_rows[GROUPS : 2 * GROUPS, :], scale_b.squeeze(0).rearrange("(j p) -> j p", p=P))
+        factor_a = held.tile([P, FEATURES], F32, name="factor_a")
         nc.scalar.dma_start(factor_a[:], scale_a.squeeze(0).partition_broadcast(P))
         nc.sync.dma_start(x_blocks[0][:], x[0:P, :])
         nc.sync.dma_start(offsets[:], offs)
-        nc.sync.dma_start(factor_b[:], scale_b.squeeze(0).partition_broadcast(P))
         for b in range(1, BLOCKS):
             nc.sync.dma_start(x_blocks[b][:], x[b * P : (b + 1) * P, :])
 
         identity = held.tile([P, P], F32, name="identity")
         make_identity(nc, identity[:])
-        a_rows = held.tile([P, P], F32, name="a_rows")
-        nc.gpsimd.memset(a_rows[:], 0.0)
-        nc.scalar.dma_start(a_rows[0 : FEATURES // P, :], scale_a.squeeze(0).rearrange("(j p) -> j p", p=P))
-        a_flipped = psum.tile([P, P], F32, name="a_flipped")
-        nc.tensor.transpose(a_flipped[:], a_rows[:], identity[:])
-        a_columns = held.tile([P, P], F32, name="a_columns")
-        nc.scalar.activation(a_columns[:], a_flipped[:], COPY)
+        rows_flipped = psum.tile([P, BANK], F32, name="rows_flipped", tag="bank")
+        nc.tensor.transpose(rows_flipped[:, 0:P], factor_rows[:], identity[:])
+        factor_columns = held.tile([P, 2 * GROUPS], F32, name="factor_columns")
+        nc.scalar.activation(factor_columns[:], rows_flipped[:, 0 : 2 * GROUPS], COPY)
+        a_columns = factor_columns[:, 0:GROUPS]
+        b_columns = factor_columns[:, GROUPS : 2 * GROUPS]
+
+        factor_b = held.tile([P, FEATURES], F32, name="factor_b")
+        for c in range(CHUNKS):
+            b_repeated = psum.tile([P, BANK], F32, name="b_repeated", tag="bank")
+            for k in range(SQUARES):
+                column = b_columns[:, c * SQUARES + k : c * SQUARES + k + 1]
+                nc.tensor.transpose(b_repeated[:, k * P : (k + 1) * P], column.to_broadcast([P, P]), identity[:])
+            nc.scalar.activation(factor_b[:, c * BANK : (c + 1) * BANK], b_repeated[:], COPY)
+
+        def flip_and_scale(x_block, c):
+            flipped = psum.tile([P, BANK], F32, name="flipped", tag="bank")
+            scaled = work.tile([P, BANK], F32, name="scaled")
+            for k in range(SQUARES):
+                j = c * SQUARES + k
+                nc.tensor.transpose(flipped[:, k * P : (k + 1) * P], x_block[:, j * P : (j + 1) * P], identity[:])
+            for k in range(SQUARES):
+                j = c * SQUARES + k
+                part = slice(k * P, (k + 1) * P)
+                nc.scalar.activation(scaled[:, part], flipped[:, part], COPY, scale=a_columns[:, j : j + 1])
+            return scaled
+
+        def flip_back(y_block, c, scaled):
+            back = psum.tile([P, BANK], F32, name="back", tag="bank")
+            for k in range(SQUARES):
+                part = slice(k * P, (k + 1) * P)
+                nc.tensor.transpose(back[:, part], scaled[:, part], identity[:])
+            nc.scalar.activation(y_block[:, c * BANK : (c + 1) * BANK], back[:], COPY)
+
+        chunks_on_vector = [CHUNKS, CHUNKS // 2, 0, 0]
 
         for b in range(BLOCKS):
             rows = slice(b * P, (b + 1) * P)
             y_block = blocks.tile([P, FEATURES], F32, name="y_block")
 
-            on_vector = 0 if b >= 2 else FEATURES
+            on_vector = chunks_on_vector[b] * BANK
             if on_vector > 0:
                 nc.vector.tensor_tensor(
                     y_block[:, 0:on_vector], x_blocks[b][:, 0:on_vector], factor_a[:, 0:on_vector], MULT
                 )
-            for start in range(on_vector, FEATURES, BANK):
-                squares = [(k, slice(k * P, (k + 1) * P), start // P + k) for k in range(SQUARES)]
-                flipped = psum.tile([P, BANK], F32, name="flipped")
-                for k, part, j in squares:
-                    nc.tensor.transpose(flipped[:, part], x_blocks[b][:, j * P : (j + 1) * P], identity[:])
-                scaled = work.tile([P, BANK], F32, name="scaled")
-                for k, part, j in squares:
-                    nc.scalar.activation(scaled[:, part], flipped[:, part], COPY, scale=a_columns[:, j : j + 1])
-                back = psum.tile([P, BANK], F32, name="back")
-                for k, part, j in squares:
-                    nc.tensor.transpose(back[:, part], scaled[:, part], identity[:])
-                nc.scalar.activation(y_block[:, start : start + BANK], back[:], COPY)
+            scaled_chunks = {}
+            for c in range(chunks_on_vector[b], CHUNKS + LAG):
+                if c < CHUNKS:
+                    scaled_chunks[c] = flip_and_scale(x_blocks[b], c)
+                if c - LAG in scaled_chunks:
+                    flip_back(y_block, c - LAG, scaled_chunks[c - LAG])
 
             out_block = blocks.tile([P, FEATURES], F32, name="out_block")
             cuts = [0, FEATURES - LAST_PIECE, FEATURES] if b == BLOCKS - 1 else [0, FEATURES]

@@ -5,7 +5,7 @@ P = 128
 TOKENS = 512
 FEATURES = 2048
 BLOCKS = TOKENS // P
-LAST_PIECE = 512
+LAST_PIECE = 256
 BANK = 512
 BANKS = 8
 CHUNKS = FEATURES // BANK
@@ -97,7 +97,11 @@ def tile_monarchlinearlayer_kernel(tc, x, scale_a, scale_b, offs, out):
                     flip_back(y_block, c - LAG, scaled_chunks[c - LAG])
 
             out_block = blocks.tile([P, FEATURES], F32, name="out_block")
-            cuts = [0, FEATURES - LAST_PIECE, FEATURES] if b == BLOCKS - 1 else [0, FEATURES]
+            cuts = [0]
+            if b == BLOCKS - 1:
+                while FEATURES - cuts[-1] > LAST_PIECE:
+                    cuts.append(cuts[-1] + (FEATURES - cuts[-1]) // 2)
+            cuts.append(FEATURES)
             for start, end in zip(cuts[:-1], cuts[1:]):
                 nc.vector.tensor_tensor(
                     out_block[:, start:end],

@@ -4,6 +4,7 @@ from concourse.masks import make_identity
 P = 128
 TOKENS = 512
 FEATURES = 2048
+HALF = FEATURES // 2
 BLOCKS = TOKENS // P
 LAST_PIECE = 256
 BANK = 512
@@ -25,7 +26,8 @@ def tile_monarchlinearlayer_kernel(tc, x, scale_a, scale_b, offs, out):
         tc.tile_pool(name="held", bufs=1) as held,
         tc.tile_pool(name="blocks", bufs=BLOCKS) as blocks,
         tc.tile_pool(name="work", bufs=LAG + 1) as work,
-        tc.psum_pool(name="psum", bufs=BANKS) as psum,
+        tc.psum_pool(name="psum_a", bufs=CHUNKS) as psum_a,
+        tc.psum_pool(name="psum", bufs=BANKS - CHUNKS) as psum,
     ):
         offsets = held.tile([P, FEATURES // 16], U16, name="offsets")
         x_blocks = [blocks.tile([P, FEATURES], F32, name="x_block") for b in range(BLOCKS)]
@@ -35,11 +37,11 @@ def tile_monarchlinearlayer_kernel(tc, x, scale_a, scale_b, offs, out):
         nc.vector.memset(factor_rows[4 * GROUPS : P, :], 0.0)
         nc.sync.dma_start(factor_rows[0:GROUPS, :], scale_a.squeeze(0).rearrange("(j p) -> j p", p=P))
         nc.scalar.dma_start(factor_rows[GROUPS : 2 * GROUPS, :], scale_b.squeeze(0).rearrange("(j p) -> j p", p=P))
-        factor_a = held.tile([P, FEATURES], F32, name="factor_a")
-        nc.scalar.dma_start(factor_a[:], scale_a.squeeze(0).partition_broadcast(P))
         nc.sync.dma_start(x_blocks[0][:], x[0:P, :])
+        nc.sync.dma_start(x_blocks[1][:, 0:HALF], x[P : 2 * P, 0:HALF])
         nc.sync.dma_start(offsets[:], offs)
-        for b in range(1, BLOCKS):
+        nc.sync.dma_start(x_blocks[1][:, HALF:FEATURES], x[P : 2 * P, HALF:FEATURES])
+        for b in range(2, BLOCKS):
             nc.sync.dma_start(x_blocks[b][:], x[b * P : (b + 1) * P, :])
 
         identity = held.tile([P, P], F32, name="identity")
@@ -51,12 +53,18 @@ def tile_monarchlinearlayer_kernel(tc, x, scale_a, scale_b, offs, out):
         a_columns = factor_columns[:, 0:GROUPS]
         b_columns = factor_columns[:, GROUPS : 2 * GROUPS]
 
+        def repeat_chunk(repeated, columns, c):
+            for k in range(SQUARES):
+                column = columns[:, c * SQUARES + k : c * SQUARES + k + 1]
+                nc.tensor.transpose(repeated[:, k * P : (k + 1) * P], column.to_broadcast([P, P]), identity[:])
+
+        a_repeated = [psum_a.tile([P, BANK], F32, name="a_repeated") for c in range(CHUNKS)]
+        for c in range(CHUNKS):
+            repeat_chunk(a_repeated[c], a_columns, c)
         factor_b = held.tile([P, FEATURES], F32, name="factor_b")
         for c in range(CHUNKS):
             b_repeated = psum.tile([P, BANK], F32, name="b_repeated", tag="bank")
-            for k in range(SQUARES):
-                column = b_columns[:, c * SQUARES + k : c * SQUARES + k + 1]
-                nc.tensor.transpose(b_repeated[:, k * P : (k + 1) * P], column.to_broadcast([P, P]), identity[:])
+            repeat_chunk(b_repeated, b_columns, c)
             nc.scalar.activation(factor_b[:, c * BANK : (c + 1) * BANK], b_repeated[:], COPY)
 
         def flip_and_scale(x_block, c):
@@ -84,11 +92,9 @@ def tile_monarchlinearlayer_kernel(tc, x, scale_a, scale_b, offs, out):
             rows = slice(b * P, (b + 1) * P)
             y_block = blocks.tile([P, FEATURES], F32, name="y_block")
 
-            on_vector = chunks_on_vector[b] * BANK
-            if on_vector > 0:
-                nc.vector.tensor_tensor(
-                    y_block[:, 0:on_vector], x_blocks[b][:, 0:on_vector], factor_a[:, 0:on_vector], MULT
-                )
+            for c in range(chunks_on_vector[b]):
+                cols = slice(c * BANK, (c + 1) * BANK)
+                nc.vector.tensor_tensor(y_block[:, cols], x_blocks[b][:, cols], a_repeated[c][:], MULT)
             scaled_chunks = {}
             for c in range(chunks_on_vector[b], CHUNKS + LAG):
                 if c < CHUNKS:
@@ -98,6 +104,8 @@ def tile_monarchlinearlayer_kernel(tc, x, scale_a, scale_b, offs, out):
 
             out_block = blocks.tile([P, FEATURES], F32, name="out_block")
             cuts = [0]
+            if b == 0:
+                cuts = [c * BANK for c in range(CHUNKS)]
             if b == BLOCKS - 1:
                 while FEATURES - cuts[-1] > LAST_PIECE:
                     cuts.append(cuts[-1] + (FEATURES - cuts[-1]) // 2)

@@ -61,6 +61,8 @@ def tile_monarchlinearlayer_kernel(tc, x, scale_a, scale_b, offs, out):
         a_repeated = [psum_a.tile([P, BANK], F32, name="a_repeated") for c in range(CHUNKS)]
         for c in range(CHUNKS):
             repeat_chunk(a_repeated[c], a_columns, c)
+        a_first = held.tile([P, BANK], F32, name="a_first")
+        nc.scalar.activation(a_first[:], a_repeated[0][:], COPY)
         factor_b = held.tile([P, FEATURES], F32, name="factor_b")
         for c in range(CHUNKS):
             b_repeated = psum.tile([P, BANK], F32, name="b_repeated", tag="bank")
@@ -86,17 +88,20 @@ def tile_monarchlinearlayer_kernel(tc, x, scale_a, scale_b, offs, out):
                 nc.tensor.transpose(back[:, part], scaled[:, part], identity[:])
             nc.scalar.activation(y_block[:, c * BANK : (c + 1) * BANK], back[:], COPY)
 
-        chunks_on_vector = [CHUNKS, CHUNKS // 2, 0, 0]
+        first_stage_done = [CHUNKS, CHUNKS // 2, 0, 0]
 
         for b in range(BLOCKS):
             rows = slice(b * P, (b + 1) * P)
             y_block = blocks.tile([P, FEATURES], F32, name="y_block")
 
-            for c in range(chunks_on_vector[b]):
+            for c in range(first_stage_done[b]):
                 cols = slice(c * BANK, (c + 1) * BANK)
-                nc.vector.tensor_tensor(y_block[:, cols], x_blocks[b][:, cols], a_repeated[c][:], MULT)
+                if c == 0:
+                    nc.gpsimd.tensor_tensor(y_block[:, cols], x_blocks[b][:, cols], a_first[:], MULT)
+                else:
+                    nc.vector.tensor_tensor(y_block[:, cols], x_blocks[b][:, cols], a_repeated[c][:], MULT)
             scaled_chunks = {}
-            for c in range(chunks_on_vector[b], CHUNKS + LAG):
+            for c in range(first_stage_done[b], CHUNKS + LAG):
                 if c < CHUNKS:
                     scaled_chunks[c] = flip_and_scale(x_blocks[b], c)
                 if c - LAG in scaled_chunks:

@@ -8,6 +8,8 @@ HALF = FEATURES // 2
 BLOCKS = TOKENS // P
 LAST_PIECE = 256
 BANK = 512
+GPSIMD_CHUNK = 0
+VECTOR_CHUNK = 1
 BANKS = 8
 CHUNKS = FEATURES // BANK
 SQUARES = BANK // P
@@ -37,7 +39,8 @@ def tile_monarchlinearlayer_kernel(tc, x, scale_a, scale_b, offs, out):
         nc.vector.memset(factor_rows[4 * GROUPS : P, :], 0.0)
         nc.sync.dma_start(factor_rows[0:GROUPS, :], scale_a.squeeze(0).rearrange("(j p) -> j p", p=P))
         nc.scalar.dma_start(factor_rows[GROUPS : 2 * GROUPS, :], scale_b.squeeze(0).rearrange("(j p) -> j p", p=P))
-        nc.sync.dma_start(x_blocks[0][:], x[0:P, :])
+        nc.sync.dma_start(x_blocks[0][:, 0:HALF], x[0:P, 0:HALF])
+        nc.sync.dma_start(x_blocks[0][:, HALF:FEATURES], x[0:P, HALF:FEATURES])
         nc.sync.dma_start(x_blocks[1][:, 0:HALF], x[P : 2 * P, 0:HALF])
         nc.sync.dma_start(offsets[:], offs)
         nc.sync.dma_start(x_blocks[1][:, HALF:FEATURES], x[P : 2 * P, HALF:FEATURES])
@@ -58,11 +61,10 @@ def tile_monarchlinearlayer_kernel(tc, x, scale_a, scale_b, offs, out):
                 column = columns[:, c * SQUARES + k : c * SQUARES + k + 1]
                 nc.tensor.transpose(repeated[:, k * P : (k + 1) * P], column.to_broadcast([P, P]), identity[:])
 
+        chunk_order = [GPSIMD_CHUNK, 2, 3, VECTOR_CHUNK]
         a_repeated = [psum_a.tile([P, BANK], F32, name="a_repeated") for c in range(CHUNKS)]
-        for c in range(CHUNKS):
+        for c in chunk_order:
             repeat_chunk(a_repeated[c], a_columns, c)
-        a_first = held.tile([P, BANK], F32, name="a_first")
-        nc.scalar.activation(a_first[:], a_repeated[0][:], COPY)
         factor_b = held.tile([P, FEATURES], F32, name="factor_b")
         for c in range(CHUNKS):
             b_repeated = psum.tile([P, BANK], F32, name="b_repeated", tag="bank")
@@ -88,21 +90,25 @@ def tile_monarchlinearlayer_kernel(tc, x, scale_a, scale_b, offs, out):
                 nc.tensor.transpose(back[:, part], scaled[:, part], identity[:])
             nc.scalar.activation(y_block[:, c * BANK : (c + 1) * BANK], back[:], COPY)
 
-        first_stage_done = [CHUNKS, CHUNKS // 2, 0, 0]
+        on_vector = [chunk_order, [VECTOR_CHUNK], [], []]
+        on_gpsimd = [[], [GPSIMD_CHUNK], [], []]
+        on_scalar = [[], [2, 3], [0, 1, 2, 3], [0, 1, 2, 3]]
 
         for b in range(BLOCKS):
             rows = slice(b * P, (b + 1) * P)
             y_block = blocks.tile([P, FEATURES], F32, name="y_block")
 
-            for c in range(first_stage_done[b]):
+            for c in on_vector[b]:
                 cols = slice(c * BANK, (c + 1) * BANK)
-                if c == 0:
-                    nc.gpsimd.tensor_tensor(y_block[:, cols], x_blocks[b][:, cols], a_first[:], MULT)
-                else:
-                    nc.vector.tensor_tensor(y_block[:, cols], x_blocks[b][:, cols], a_repeated[c][:], MULT)
+                nc.vector.tensor_tensor(y_block[:, cols], x_blocks[b][:, cols], a_repeated[c][:], MULT)
+            for c in on_gpsimd[b]:
+                cols = slice(c * BANK, (c + 1) * BANK)
+                a_in_sbuf = held.tile([P, BANK], F32, name="a_in_sbuf")
+                nc.scalar.activation(a_in_sbuf[:], a_repeated[c][:], COPY)
+                nc.gpsimd.tensor_tensor(y_block[:, cols], x_blocks[b][:, cols], a_in_sbuf[:], MULT)
             scaled_chunks = {}
-            for c in range(first_stage_done[b], CHUNKS + LAG):
-                if c < CHUNKS:
+            for c in range(CHUNKS + LAG):
+                if c in on_scalar[b]:
                     scaled_chunks[c] = flip_and_scale(x_blocks[b], c)
                 if c - LAG in scaled_chunks:
                     flip_back(y_block, c - LAG, scaled_chunks[c - LAG])

@@ -14,7 +14,7 @@ BANKS = 8
 CHUNKS = FEATURES // BANK
 SQUARES = BANK // P
 GROUPS = FEATURES // P
-LAG = 2
+LAG = 3
 
 F32 = mybir.dt.float32
 U16 = mybir.dt.uint16
@@ -28,8 +28,7 @@ def tile_monarchlinearlayer_kernel(tc, x, scale_a, scale_b, offs, out):
         tc.tile_pool(name="held", bufs=1) as held,
         tc.tile_pool(name="blocks", bufs=BLOCKS) as blocks,
         tc.tile_pool(name="work", bufs=LAG + 1) as work,
-        tc.psum_pool(name="psum_a", bufs=CHUNKS) as psum_a,
-        tc.psum_pool(name="psum", bufs=BANKS - CHUNKS) as psum,
+        tc.psum_pool(name="psum", bufs=BANKS) as psum,
     ):
         offsets = held.tile([P, FEATURES // 16], U16, name="offsets")
         x_blocks = [blocks.tile([P, FEATURES], F32, name="x_block") for b in range(BLOCKS)]
@@ -62,7 +61,7 @@ def tile_monarchlinearlayer_kernel(tc, x, scale_a, scale_b, offs, out):
                 nc.tensor.transpose(repeated[:, k * P : (k + 1) * P], column.to_broadcast([P, P]), identity[:])
 
         chunk_order = [GPSIMD_CHUNK, 2, 3, VECTOR_CHUNK]
-        a_repeated = [psum_a.tile([P, BANK], F32, name="a_repeated") for c in range(CHUNKS)]
+        a_repeated = [psum.tile([P, BANK], F32, name="a_repeated", tag="bank") for c in range(CHUNKS)]
         for c in chunk_order:
             repeat_chunk(a_repeated[c], a_columns, c)
         factor_b = held.tile([P, FEATURES], F32, name="factor_b")

@@ -8,13 +8,11 @@ HALF = FEATURES // 2
 BLOCKS = TOKENS // P
 LAST_PIECE = 256
 BANK = 512
-GPSIMD_CHUNK = 0
-VECTOR_CHUNK = 1
 BANKS = 8
 CHUNKS = FEATURES // BANK
 SQUARES = BANK // P
 GROUPS = FEATURES // P
-LAG = 3
+LAG = 2
 
 F32 = mybir.dt.float32
 U16 = mybir.dt.uint16
@@ -40,7 +38,8 @@ def tile_monarchlinearlayer_kernel(tc, x, scale_a, scale_b, offs, out):
         nc.scalar.dma_start(factor_rows[GROUPS : 2 * GROUPS, :], scale_b.squeeze(0).rearrange("(j p) -> j p", p=P))
         nc.sync.dma_start(x_blocks[0][:, 0:HALF], x[0:P, 0:HALF])
         nc.sync.dma_start(x_blocks[0][:, HALF:FEATURES], x[0:P, HALF:FEATURES])
-        nc.sync.dma_start(x_blocks[1][:, 0:HALF], x[P : 2 * P, 0:HALF])
+        for cols in (slice(0, BANK), slice(BANK, HALF)):
+            nc.sync.dma_start(x_blocks[1][:, cols], x[P : 2 * P, cols])
         nc.sync.dma_start(offsets[:], offs)
         nc.sync.dma_start(x_blocks[1][:, HALF:FEATURES], x[P : 2 * P, HALF:FEATURES])
         for b in range(2, BLOCKS):
@@ -51,24 +50,38 @@ def tile_monarchlinearlayer_kernel(tc, x, scale_a, scale_b, offs, out):
         rows_flipped = psum.tile([P, BANK], F32, name="rows_flipped", tag="bank")
         nc.tensor.transpose(rows_flipped[:, 0:P], factor_rows[:], identity[:])
         factor_columns = held.tile([P, 2 * GROUPS], F32, name="factor_columns")
-        nc.scalar.activation(factor_columns[:], rows_flipped[:, 0 : 2 * GROUPS], COPY)
+        nc.vector.tensor_copy(factor_columns[:], rows_flipped[:, 0 : 2 * GROUPS])
         a_columns = factor_columns[:, 0:GROUPS]
         b_columns = factor_columns[:, GROUPS : 2 * GROUPS]
 
-        def repeat_chunk(repeated, columns, c):
-            for k in range(SQUARES):
-                column = columns[:, c * SQUARES + k : c * SQUARES + k + 1]
+        def repeat(columns, cols):
+            repeated = psum.tile([P, BANK], F32, name="repeated", tag="bank")
+            for k in range((cols.stop - cols.start) // P):
+                j = cols.start // P + k
+                column = columns[:, j : j + 1]
                 nc.tensor.transpose(repeated[:, k * P : (k + 1) * P], column.to_broadcast([P, P]), identity[:])
+            return repeated[:, 0 : cols.stop - cols.start]
 
-        chunk_order = [GPSIMD_CHUNK, 2, 3, VECTOR_CHUNK]
-        a_repeated = [psum.tile([P, BANK], F32, name="a_repeated", tag="bank") for c in range(CHUNKS)]
-        for c in chunk_order:
-            repeat_chunk(a_repeated[c], a_columns, c)
+        chunks = [slice(c * BANK, (c + 1) * BANK) for c in range(CHUNKS)]
+        first_chunk_halves = [slice(0, BANK // 2), slice(BANK // 2, BANK)]
+
+        a_pieces = first_chunk_halves + [chunks[2], chunks[3], chunks[1]]
+        a_repeated = [repeat(a_columns, cols) for cols in a_pieces]
+
+        y_blocks = [blocks.tile([P, FEATURES], F32, name="y_block") for b in range(BLOCKS)]
+        for b, pieces_on_vector in ((0, len(a_pieces)), (1, 1)):
+            for i in range(len(a_pieces) - pieces_on_vector, len(a_pieces)):
+                cols = a_pieces[i]
+                nc.vector.tensor_tensor(y_blocks[b][:, cols], x_blocks[b][:, cols], a_repeated[i], MULT)
+        a_in_sbuf = held.tile([P, BANK], F32, name="a_in_sbuf")
+        for i, cols in enumerate(first_chunk_halves):
+            nc.scalar.activation(a_in_sbuf[:, cols], a_repeated[i], COPY)
+        nc.gpsimd.tensor_tensor(y_blocks[1][:, 0:BANK], x_blocks[1][:, 0:BANK], a_in_sbuf[:], MULT)
+
         factor_b = held.tile([P, FEATURES], F32, name="factor_b")
-        for c in range(CHUNKS):
-            b_repeated = psum.tile([P, BANK], F32, name="b_repeated", tag="bank")
-            repeat_chunk(b_repeated, b_columns, c)
-            nc.scalar.activation(factor_b[:, c * BANK : (c + 1) * BANK], b_repeated[:], COPY)
+        b_pieces = first_chunk_halves + chunks[1:]
+        for cols in b_pieces:
+            nc.scalar.activation(factor_b[:, cols], repeat(b_columns, cols), COPY)
 
         def flip_and_scale(x_block, c):
             flipped = psum.tile([P, BANK], F32, name="flipped", tag="bank")
@@ -89,22 +102,10 @@ def tile_monarchlinearlayer_kernel(tc, x, scale_a, scale_b, offs, out):
                 nc.tensor.transpose(back[:, part], scaled[:, part], identity[:])
             nc.scalar.activation(y_block[:, c * BANK : (c + 1) * BANK], back[:], COPY)
 
-        on_vector = [chunk_order, [VECTOR_CHUNK], [], []]
-        on_gpsimd = [[], [GPSIMD_CHUNK], [], []]
         on_scalar = [[], [2, 3], [0, 1, 2, 3], [0, 1, 2, 3]]
-
         for b in range(BLOCKS):
             rows = slice(b * P, (b + 1) * P)
-            y_block = blocks.tile([P, FEATURES], F32, name="y_block")
-
-            for c in on_vector[b]:
-                cols = slice(c * BANK, (c + 1) * BANK)
-                nc.vector.tensor_tensor(y_block[:, cols], x_blocks[b][:, cols], a_repeated[c][:], MULT)
-            for c in on_gpsimd[b]:
-                cols = slice(c * BANK, (c + 1) * BANK)
-                a_in_sbuf = held.tile([P, BANK], F32, name="a_in_sbuf")
-                nc.scalar.activation(a_in_sbuf[:], a_repeated[c][:], COPY)
-                nc.gpsimd.tensor_tensor(y_block[:, cols], x_blocks[b][:, cols], a_in_sbuf[:], MULT)
+            y_block = y_blocks[b]
             scaled_chunks = {}
             for c in range(CHUNKS + LAG):
                 if c in on_scalar[b]:
@@ -115,7 +116,7 @@ def tile_monarchlinearlayer_kernel(tc, x, scale_a, scale_b, offs, out):
             out_block = blocks.tile([P, FEATURES], F32, name="out_block")
             cuts = [0]
             if b == 0:
-                cuts = [c * BANK for c in range(CHUNKS)]
+                cuts = [cols.start for cols in b_pieces]
             if b == BLOCKS - 1:
                 while FEATURES - cuts[-1] > LAST_PIECE:
                     cuts.append(cuts[-1] + (FEATURES - cuts[-1]) // 2)

@@ -38,10 +38,10 @@ def tile_monarchlinearlayer_kernel(tc, x, scale_a, scale_b, offs, out):
         nc.scalar.dma_start(factor_rows[GROUPS : 2 * GROUPS, :], scale_b.squeeze(0).rearrange("(j p) -> j p", p=P))
         nc.sync.dma_start(x_blocks[0][:, 0:HALF], x[0:P, 0:HALF])
         nc.sync.dma_start(x_blocks[0][:, HALF:FEATURES], x[0:P, HALF:FEATURES])
-        for cols in (slice(0, BANK), slice(BANK, HALF)):
+        for cols in (slice(0, BANK), slice(FEATURES - BANK, FEATURES)):
             nc.sync.dma_start(x_blocks[1][:, cols], x[P : 2 * P, cols])
         nc.sync.dma_start(offsets[:], offs)
-        nc.sync.dma_start(x_blocks[1][:, HALF:FEATURES], x[P : 2 * P, HALF:FEATURES])
+        nc.sync.dma_start(x_blocks[1][:, BANK : FEATURES - BANK], x[P : 2 * P, BANK : FEATURES - BANK])
         for b in range(2, BLOCKS):
             nc.sync.dma_start(x_blocks[b][:], x[b * P : (b + 1) * P, :])
 
@@ -65,7 +65,7 @@ def tile_monarchlinearlayer_kernel(tc, x, scale_a, scale_b, offs, out):
         chunks = [slice(c * BANK, (c + 1) * BANK) for c in range(CHUNKS)]
         first_chunk_halves = [slice(0, BANK // 2), slice(BANK // 2, BANK)]
 
-        a_pieces = first_chunk_halves + [chunks[2], chunks[3], chunks[1]]
+        a_pieces = first_chunk_halves + chunks[1:]
         a_repeated = [repeat(a_columns, cols) for cols in a_pieces]
 
         y_blocks = [blocks.tile([P, FEATURES], F32, name="y_block") for b in range(BLOCKS)]
@@ -102,7 +102,7 @@ def tile_monarchlinearlayer_kernel(tc, x, scale_a, scale_b, offs, out):
                 nc.tensor.transpose(back[:, part], scaled[:, part], identity[:])
             nc.scalar.activation(y_block[:, c * BANK : (c + 1) * BANK], back[:], COPY)
 
-        on_scalar = [[], [2, 3], [0, 1, 2, 3], [0, 1, 2, 3]]
+        on_scalar = [[], [1, 2], [0, 1, 2, 3], [0, 1, 2, 3]]
         for b in range(BLOCKS):
             rows = slice(b * P, (b + 1) * P)
             y_block = y_blocks[b]

@@ -36,8 +36,8 @@ def tile_monarchlinearlayer_kernel(tc, x, scale_a, scale_b, offs, out):
         nc.vector.memset(factor_rows[4 * GROUPS : P, :], 0.0)
         nc.sync.dma_start(factor_rows[0:GROUPS, :], scale_a.squeeze(0).rearrange("(j p) -> j p", p=P))
         nc.scalar.dma_start(factor_rows[GROUPS : 2 * GROUPS, :], scale_b.squeeze(0).rearrange("(j p) -> j p", p=P))
-        nc.sync.dma_start(x_blocks[0][:, 0:HALF], x[0:P, 0:HALF])
-        nc.sync.dma_start(x_blocks[0][:, HALF:FEATURES], x[0:P, HALF:FEATURES])
+        for cols in (slice(0, BANK), slice(BANK, HALF), slice(HALF, FEATURES)):
+            nc.sync.dma_start(x_blocks[0][:, cols], x[0:P, cols])
         for cols in (slice(0, BANK), slice(FEATURES - BANK, FEATURES)):
             nc.sync.dma_start(x_blocks[1][:, cols], x[P : 2 * P, cols])
         nc.sync.dma_start(offsets[:], offs)

@@ -6,8 +6,9 @@ TOKENS = 512
 FEATURES = 2048
 HALF = FEATURES // 2
 BLOCKS = TOKENS // P
-LAST_PIECE = 256
+LAST_PIECE = 128
 BANK = 512
+HALF_BANK = BANK // 2
 BANKS = 8
 CHUNKS = FEATURES // BANK
 SQUARES = BANK // P
@@ -38,10 +39,10 @@ def tile_monarchlinearlayer_kernel(tc, x, scale_a, scale_b, offs, out):
         nc.scalar.dma_start(factor_rows[GROUPS : 2 * GROUPS, :], scale_b.squeeze(0).rearrange("(j p) -> j p", p=P))
         for cols in (slice(0, BANK), slice(BANK, HALF), slice(HALF, FEATURES)):
             nc.sync.dma_start(x_blocks[0][:, cols], x[0:P, cols])
-        for cols in (slice(0, BANK), slice(FEATURES - BANK, FEATURES)):
+        for cols in (slice(0, BANK), slice(FEATURES - HALF_BANK, FEATURES)):
             nc.sync.dma_start(x_blocks[1][:, cols], x[P : 2 * P, cols])
         nc.sync.dma_start(offsets[:], offs)
-        nc.sync.dma_start(x_blocks[1][:, BANK : FEATURES - BANK], x[P : 2 * P, BANK : FEATURES - BANK])
+        nc.sync.dma_start(x_blocks[1][:, BANK : FEATURES - HALF_BANK], x[P : 2 * P, BANK : FEATURES - HALF_BANK])
         for b in range(2, BLOCKS):
             nc.sync.dma_start(x_blocks[b][:], x[b * P : (b + 1) * P, :])
 
@@ -63,16 +64,17 @@ def tile_monarchlinearlayer_kernel(tc, x, scale_a, scale_b, offs, out):
             return repeated[:, 0 : cols.stop - cols.start]
 
         chunks = [slice(c * BANK, (c + 1) * BANK) for c in range(CHUNKS)]
-        first_chunk_halves = [slice(0, BANK // 2), slice(BANK // 2, BANK)]
+        first_chunk_halves = [slice(0, HALF_BANK), slice(HALF_BANK, BANK)]
 
-        a_pieces = first_chunk_halves + chunks[1:]
+        last_chunk_halves = [slice(FEATURES - BANK, FEATURES - HALF_BANK), slice(FEATURES - HALF_BANK, FEATURES)]
+        a_pieces = first_chunk_halves + chunks[1:3] + last_chunk_halves
         a_repeated = [repeat(a_columns, cols) for cols in a_pieces]
 
         y_blocks = [blocks.tile([P, FEATURES], F32, name="y_block") for b in range(BLOCKS)]
-        for b, pieces_on_vector in ((0, len(a_pieces)), (1, 1)):
-            for i in range(len(a_pieces) - pieces_on_vector, len(a_pieces)):
-                cols = a_pieces[i]
-                nc.vector.tensor_tensor(y_blocks[b][:, cols], x_blocks[b][:, cols], a_repeated[i], MULT)
+        for cols, factors in zip(a_pieces, a_repeated):
+            nc.vector.tensor_tensor(y_blocks[0][:, cols], x_blocks[0][:, cols], factors, MULT)
+        cols = a_pieces[-1]
+        nc.vector.tensor_tensor(y_blocks[1][:, cols], x_blocks[1][:, cols], a_repeated[-1], MULT)
         a_in_sbuf = held.tile([P, BANK], F32, name="a_in_sbuf")
         for i, cols in enumerate(first_chunk_halves):
             nc.scalar.activation(a_in_sbuf[:, cols], a_repeated[i], COPY)
@@ -83,40 +85,43 @@ def tile_monarchlinearlayer_kernel(tc, x, scale_a, scale_b, offs, out):
         for cols in b_pieces:
             nc.scalar.activation(factor_b[:, cols], repeat(b_columns, cols), COPY)
 
-        def flip_and_scale(x_block, c):
+        def flip_and_scale(x_block, cols):
             flipped = psum.tile([P, BANK], F32, name="flipped", tag="bank")
             scaled = work.tile([P, BANK], F32, name="scaled")
-            for k in range(SQUARES):
-                j = c * SQUARES + k
+            squares = range((cols.stop - cols.start) // P)
+            for k in squares:
+                j = cols.start // P + k
                 nc.tensor.transpose(flipped[:, k * P : (k + 1) * P], x_block[:, j * P : (j + 1) * P], identity[:])
-            for k in range(SQUARES):
-                j = c * SQUARES + k
+            for k in squares:
+                j = cols.start // P + k
                 part = slice(k * P, (k + 1) * P)
                 nc.scalar.activation(scaled[:, part], flipped[:, part], COPY, scale=a_columns[:, j : j + 1])
             return scaled
 
-        def flip_back(y_block, c, scaled):
+        def flip_back(y_block, cols, scaled):
+            width = cols.stop - cols.start
             back = psum.tile([P, BANK], F32, name="back", tag="bank")
-            for k in range(SQUARES):
+            for k in range(width // P):
                 part = slice(k * P, (k + 1) * P)
                 nc.tensor.transpose(back[:, part], scaled[:, part], identity[:])
-            nc.scalar.activation(y_block[:, c * BANK : (c + 1) * BANK], back[:], COPY)
+            nc.scalar.activation(y_block[:, cols], back[:, 0:width], COPY)
 
-        on_scalar = [[], [1, 2], [0, 1, 2, 3], [0, 1, 2, 3]]
+        on_scalar = [[], chunks[1:3] + last_chunk_halves[:1], chunks, chunks]
         for b in range(BLOCKS):
             rows = slice(b * P, (b + 1) * P)
             y_block = y_blocks[b]
-            scaled_chunks = {}
-            for c in range(CHUNKS + LAG):
-                if c in on_scalar[b]:
-                    scaled_chunks[c] = flip_and_scale(x_blocks[b], c)
-                if c - LAG in scaled_chunks:
-                    flip_back(y_block, c - LAG, scaled_chunks[c - LAG])
+            pieces = on_scalar[b]
+            scaled_pieces = []
+            for i in range(len(pieces) + LAG):
+                if i < len(pieces):
+                    scaled_pieces.append(flip_and_scale(x_blocks[b], pieces[i]))
+                if i >= LAG:
+                    flip_back(y_block, pieces[i - LAG], scaled_pieces[i - LAG])
 
             out_block = blocks.tile([P, FEATURES], F32, name="out_block")
             cuts = [0]
             if b == 0:
-                cuts = [cols.start for cols in b_pieces]
+                cuts = [cols.start for cols in b_pieces[:-1]]
             if b == BLOCKS - 1:
                 while FEATURES - cuts[-1] > LAST_PIECE:
                     cuts.append(cuts[-1] + (FEATURES - cuts[-1]) // 2)

import concourse.mybir as mybir
from concourse.masks import make_identity

P = 128
TOKENS = 512
FEATURES = 2048
HALF = FEATURES // 2
BLOCKS = TOKENS // P
LAST_PIECE = 128
BANK = 512
HALF_BANK = BANK // 2
BANKS = 8
CHUNKS = FEATURES // BANK
SQUARES = BANK // P
GROUPS = FEATURES // P
LAG = 2

F32 = mybir.dt.float32
U16 = mybir.dt.uint16
MULT = mybir.AluOpType.mult
COPY = mybir.ActivationFunctionType.Copy


def tile_monarchlinearlayer_kernel(tc, x, scale_a, scale_b, offs, out):
    nc = tc.nc
    with (
        tc.tile_pool(name="held", bufs=1) as held,
        tc.tile_pool(name="blocks", bufs=BLOCKS) as blocks,
        tc.tile_pool(name="work", bufs=LAG + 1) as work,
        tc.psum_pool(name="psum", bufs=BANKS) as psum,
    ):
        offsets = held.tile([P, FEATURES // 16], U16, name="offsets")
        x_blocks = [blocks.tile([P, FEATURES], F32, name="x_block") for b in range(BLOCKS)]

        factor_rows = held.tile([P, P], F32, name="factor_rows")
        nc.vector.memset(factor_rows[2 * GROUPS : 4 * GROUPS, :], 0.0)
        nc.vector.memset(factor_rows[4 * GROUPS : P, :], 0.0)
        nc.sync.dma_start(factor_rows[0:GROUPS, :], scale_a.squeeze(0).rearrange("(j p) -> j p", p=P))
        nc.scalar.dma_start(factor_rows[GROUPS : 2 * GROUPS, :], scale_b.squeeze(0).rearrange("(j p) -> j p", p=P))
        for cols in (slice(0, BANK), slice(BANK, HALF), slice(HALF, FEATURES)):
            nc.sync.dma_start(x_blocks[0][:, cols], x[0:P, cols])
        for cols in (slice(0, BANK), slice(FEATURES - HALF_BANK, FEATURES)):
            nc.sync.dma_start(x_blocks[1][:, cols], x[P : 2 * P, cols])
        nc.sync.dma_start(offsets[:], offs)
        nc.sync.dma_start(x_blocks[1][:, BANK : FEATURES - HALF_BANK], x[P : 2 * P, BANK : FEATURES - HALF_BANK])
        for b in range(2, BLOCKS):
            nc.sync.dma_start(x_blocks[b][:], x[b * P : (b + 1) * P, :])

        identity = held.tile([P, P], F32, name="identity")
        make_identity(nc, identity[:])
        rows_flipped = psum.tile([P, BANK], F32, name="rows_flipped", tag="bank")
        nc.tensor.transpose(rows_flipped[:, 0:P], factor_rows[:], identity[:])
        factor_columns = held.tile([P, 2 * GROUPS], F32, name="factor_columns")
        nc.vector.tensor_copy(factor_columns[:], rows_flipped[:, 0 : 2 * GROUPS])
        a_columns = factor_columns[:, 0:GROUPS]
        b_columns = factor_columns[:, GROUPS : 2 * GROUPS]

        def repeat(columns, cols):
            repeated = psum.tile([P, BANK], F32, name="repeated", tag="bank")
            for k in range((cols.stop - cols.start) // P):
                j = cols.start // P + k
                column = columns[:, j : j + 1]
                nc.tensor.transpose(repeated[:, k * P : (k + 1) * P], column.to_broadcast([P, P]), identity[:])
            return repeated[:, 0 : cols.stop - cols.start]

        chunks = [slice(c * BANK, (c + 1) * BANK) for c in range(CHUNKS)]
        first_chunk_halves = [slice(0, HALF_BANK), slice(HALF_BANK, BANK)]

        last_chunk_halves = [slice(FEATURES - BANK, FEATURES - HALF_BANK), slice(FEATURES - HALF_BANK, FEATURES)]
        a_pieces = first_chunk_halves + chunks[1:3] + last_chunk_halves
        a_repeated = [repeat(a_columns, cols) for cols in a_pieces]

        y_blocks = [blocks.tile([P, FEATURES], F32, name="y_block") for b in range(BLOCKS)]
        for cols, factors in zip(a_pieces, a_repeated):
            nc.vector.tensor_tensor(y_blocks[0][:, cols], x_blocks[0][:, cols], factors, MULT)
        cols = a_pieces[-1]
        nc.vector.tensor_tensor(y_blocks[1][:, cols], x_blocks[1][:, cols], a_repeated[-1], MULT)
        a_in_sbuf = held.tile([P, BANK], F32, name="a_in_sbuf")
        for i, cols in enumerate(first_chunk_halves):
            nc.scalar.activation(a_in_sbuf[:, cols], a_repeated[i], COPY)
        nc.gpsimd.tensor_tensor(y_blocks[1][:, 0:BANK], x_blocks[1][:, 0:BANK], a_in_sbuf[:], MULT)

        factor_b = held.tile([P, FEATURES], F32, name="factor_b")
        b_pieces = first_chunk_halves + chunks[1:]
        for cols in b_pieces:
            nc.scalar.activation(factor_b[:, cols], repeat(b_columns, cols), COPY)

        def flip_and_scale(x_block, cols):
            flipped = psum.tile([P, BANK], F32, name="flipped", tag="bank")
            scaled = work.tile([P, BANK], F32, name="scaled")
            squares = range((cols.stop - cols.start) // P)
            for k in squares:
                j = cols.start // P + k
                nc.tensor.transpose(flipped[:, k * P : (k + 1) * P], x_block[:, j * P : (j + 1) * P], identity[:])
            for k in squares:
                j = cols.start // P + k
                part = slice(k * P, (k + 1) * P)
                nc.scalar.activation(scaled[:, part], flipped[:, part], COPY, scale=a_columns[:, j : j + 1])
            return scaled

        def flip_back(y_block, cols, scaled):
            width = cols.stop - cols.start
            back = psum.tile([P, BANK], F32, name="back", tag="bank")
            for k in range(width // P):
                part = slice(k * P, (k + 1) * P)
                nc.tensor.transpose(back[:, part], scaled[:, part], identity[:])
            nc.scalar.activation(y_block[:, cols], back[:, 0:width], COPY)

        on_scalar = [[], chunks[1:3] + last_chunk_halves[:1], chunks, chunks]
        for b in range(BLOCKS):
            rows = slice(b * P, (b + 1) * P)
            y_block = y_blocks[b]
            pieces = on_scalar[b]
            scaled_pieces = []
            for i in range(len(pieces) + LAG):
                if i < len(pieces):
                    scaled_pieces.append(flip_and_scale(x_blocks[b], pieces[i]))
                if i >= LAG:
                    flip_back(y_block, pieces[i - LAG], scaled_pieces[i - LAG])

            out_block = blocks.tile([P, FEATURES], F32, name="out_block")
            cuts = [0]
            if b == 0:
                cuts = [cols.start for cols in b_pieces[:-1]]
            if b == BLOCKS - 1:
                while FEATURES - cuts[-1] > LAST_PIECE:
                    cuts.append(cuts[-1] + (FEATURES - cuts[-1]) // 2)
            cuts.append(FEATURES)
            for start, end in zip(cuts[:-1], cuts[1:]):
                nc.vector.tensor_tensor(
                    out_block[:, start:end],
                    y_block[:].indirect(offsets[:, start // 16 : end // 16]),
                    factor_b[:, start:end],
                    MULT,
                )
                nc.sync.dma_start(out[rows, start:end], out_block[:, start:end])
